import numpy as np
import ml_dtypes


def mxq(x, axis, fmt="e4m3"):
    dtype, down = {"e4m3": (ml_dtypes.float8_e4m3fn, 7), "e5m2": (ml_dtypes.float8_e5m2, 14)}[fmt]
    v = np.moveaxis(np.asarray(x, np.float32).astype(ml_dtypes.bfloat16).astype(np.float64), axis, -1)
    blocks = v.reshape(v.shape[:-1] + (-1, 32))
    amax = np.abs(blocks).max(-1, keepdims=True)
    byte = np.maximum(np.where(amax > 0, np.frexp(amax)[1] - 1 + 127, 0) - down, 1)
    scale = np.exp2(byte - 127.0)
    codes = (blocks / scale).astype(np.float32).astype(dtype).astype(np.float64)
    return np.moveaxis((codes * scale).reshape(v.shape), -1, axis)


WIDE = False


def mx_kscale(k):
    if not WIDE:
        return np.ones(k)
    levels = np.array([10, -10, 5, -5, 0])
    if k % 512:
        return np.exp2(np.random.permutation(np.resize(levels, k // 32))).repeat(32)
    a = np.empty((k // 512, 16))
    for p in range(k // 512):
        a[p, :8] = np.random.permutation(np.resize(levels, 8))
        for g in range(8):
            far = levels[np.abs(levels - a[p, g]) >= 10]
            a[p, g + 8] = far[np.random.randint(len(far))]
    return np.exp2(a.ravel()).repeat(32)


BF16 = ml_dtypes.bfloat16


def bf(x):
    return np.asarray(x, np.float32).astype(BF16)


def f64(x):
    return np.asarray(x).astype(np.float64)


H, D, L = 4, 1024, 512
HD = H * D


def split_heads(x):
    return x.reshape(L, H, D).transpose(1, 2, 0)


def setup_inputs():
    s, t = mx_kscale(D), mx_kscale(L)
    tr = np.repeat(t, HD // L)
    e = np.exp(1.5 * np.random.standard_normal((H, L, L)))
    return {"attn": bf(e / e.sum(0, keepdims=True) / t),
            "tokens": bf(np.random.standard_normal((D, L)) * s[:, None]),
            "Wv": bf(np.random.standard_normal((HD, D)) * 0.5 / np.sqrt(D) / s * tr[:, None]),
            "bv": bf(np.random.standard_normal(HD) * 0.15 * tr)}


def reference(attn, tokens, Wv, bv):
    v = split_heads((mxq(f64(Wv), 1, "e4m3") @ mxq(f64(tokens), 0, "e4m3")) + f64(bv)[:, None])
    return mxq(v, 2, "e4m3") @ mxq(f64(attn).transpose(0, 2, 1), 1, "e4m3")

@@ -1,0 +1,290 @@
+from contextlib import ExitStack
+
+import concourse.mybir as mybir
+from concourse.masks import make_identity
+
+F32 = mybir.dt.float32
+BF16 = mybir.dt.bfloat16
+U32 = mybir.dt.uint32
+U8 = mybir.dt.uint8
+FP8X4 = mybir.dt.float8_e4m3fn_x4
+ADD = mybir.AluOpType.add
+
+P = 128
+FLOPS = 2 * 4096 * 1024 * 512 + 2 * 4 * 1024 * 512 * 512
+
+
+def tile_selfattention_pb_kernel(tc, attn, tokens, Wv, bv, out):
+    nc = tc.nc
+    tok_v = tokens.rearrange("(g q s) c -> g q (s c)", g=2, q=P, s=4)
+    w_v = Wv.rearrange("(p u e j) k -> j u p e k", u=2, p=P, e=2, j=8)
+    attn_v = attn.rearrange("h (p s) m -> h p (s m)", s=4)
+    bv_v = bv.rearrange("(p x) -> p x", p=P, x=32)
+    out_v = out.rearrange("h (d i c) l -> h d i (c l)", d=2, i=P, c=4)
+
+    with ExitStack() as ctx:
+        keep = ctx.enter_context(tc.tile_pool(name="keep", bufs=1))
+        wraw_pool = ctx.enter_context(tc.tile_pool(name="wraw", bufs=8))
+        araw_pool = ctx.enter_context(tc.tile_pool(name="araw", bufs=4))
+        two = ctx.enter_context(tc.tile_pool(name="two", bufs=2))
+        outp = ctx.enter_context(tc.tile_pool(name="outp", bufs=3))
+        psum = ctx.enter_context(tc.psum_pool(name="psum", bufs=8))
+        ctx.enter_context(tc.manual_schedule())
+
+        braw = keep.tile([P, 32], BF16, name="braw")
+        nc.scalar.dma_start(out=braw[:], in_=bv_v)
+        traw = keep.tile([P, 4096], BF16, name="traw")
+        for g in range(2):
+            nc.sync.dma_start(
+                out=traw[:, g * 2048:(g + 1) * 2048],
+                in_=tok_v[g],
+            )
+        wraw = {}
+        araw = {}
+
+        def load_w(j):
+            wraw[j] = wraw_pool.tile([P, 4096], BF16, name="wraw", tag="wraw")
+            for u in range(2):
+                if j == 0:
+                    for e in range(2):
+                        t = 2 * u + e
+                        nc.sync.dma_start(out=wraw[j][:, t * 1024:(t + 1) * 1024], in_=w_v[j, u][:, e, :])
+                else:
+                    nc.sync.dma_start(
+                        out=wraw[j][:, u * 2048:(u + 1) * 2048].rearrange("p (e k) -> p e k", e=2),
+                        in_=w_v[j, u],
+                    )
+
+        def load_a(h):
+            araw[h] = araw_pool.tile([P, 2048], BF16, name="araw", tag="araw")
+            nc.sync.dma_start(out=araw[h][:], in_=attn_v[h])
+
+        load_w(0)
+        load_w(1)
+        load_a(0)
+        load_w(2)
+        load_w(3)
+        load_a(1)
+        load_w(4)
+        load_w(5)
+        load_a(2)
+        load_w(6)
+        load_w(7)
+        load_a(3)
+
+        ident = keep.tile([P, P], F32, name="ident")
+        make_identity(nc, ident[:])
+
+        tgrp = keep.tile([P, 4096], BF16, name="tgrp", align_bytes=64)
+        tcod = keep.tile([P, 1024], U32, name="tcod", align_bytes=64)
+        tscl = keep.tile([P, 1024], U8, name="tscl", align_bytes=64)
+        def regroup(copy, g, k0, nk):
+            copy(
+                out=tgrp[:, g * 2048 + k0 * 512:g * 2048 + (k0 + nk) * 512].rearrange(
+                    "q (k i t) -> q k i t", k=nk, i=P, t=4),
+                in_=traw[:, g * 2048:(g + 1) * 2048].rearrange(
+                    "q (t i k) -> q k i t", t=4, i=P, k=4)[:, k0:k0 + nk],
+            )
+
+        regroup(nc.vector.tensor_copy, 0, 0, 4)
+        regroup(nc.vector.tensor_copy, 1, 0, 2)
+        regroup(nc.scalar.copy, 1, 2, 2)
+        for g in range(2):
+            nc.vector.quantize_mx(
+                out=tcod[:, g * 512:(g + 1) * 512].bitcast(FP8X4),
+                scales=tscl[:, g * 512:(g + 1) * 512],
+                in_=tgrp[:, g * 2048:(g + 1) * 2048],
+            )
+        biasf = keep.tile([P, 32], F32, name="biasf")
+        nc.vector.tensor_copy(
+            out=biasf[:].rearrange("p (j t) -> p j t", t=4),
+            in_=braw[:].rearrange("p (t j) -> p j t", t=4),
+        )
+
+        wgrp = {}
+        wcod = {}
+        wscl = {}
+        agrp = {}
+        acod = {}
+        ascl = {}
+        vgrp = {}
+        vcod = {}
+        vscl = {}
+        osb = {}
+
+        def trans_w(j):
+            wgrp[j] = two.tile([P, 4096], BF16, name="wgrp", tag="wgrp", align_bytes=64)
+            w32 = wraw[j][:].bitcast(F32)
+            g32 = wgrp[j][:].bitcast(F32)
+            for t in range(4):
+                bank = psum.tile([P, 512], F32, name="bank", tag="bank")
+                for x in range(4):
+                    w0 = t * 512 + (x // 2) * 256
+                    nc.tensor.transpose(
+                        bank[:, x * P:(x + 1) * P],
+                        w32[:, w0 + x % 2:w0 + 256:2],
+                        ident[:],
+                    )
+                nc.scalar.copy(
+                    out=g32[:, t * 512:(t + 1) * 512].rearrange("p (g c a) -> p g c a", g=2, c=P, a=2),
+                    in_=bank[:].rearrange("p (g a c) -> p g c a", g=2, a=2, c=P),
+                )
+
+        def quant_w(j, t0, nt):
+            if t0 == 0:
+                wcod[j] = two.tile([P, 1024], U32, name="wcod", tag="wcod", align_bytes=64)
+                wscl[j] = two.tile([P, 1024], U8, name="wscl", tag="wscl", align_bytes=64)
+            nc.vector.quantize_mx(
+                out=wcod[j][:, t0 * 256:(t0 + nt) * 256].bitcast(FP8X4),
+                scales=wscl[j][:, t0 * 256:(t0 + nt) * 256],
+                in_=wgrp[j][:, t0 * 1024:(t0 + nt) * 1024],
+            )
+
+        def trans_a(h, half):
+            if half == 0:
+                agrp[h] = two.tile([P, 2048], BF16, name="agrp", tag="agrp", align_bytes=64)
+            a32 = araw[h][:].bitcast(F32)
+            g32 = agrp[h][:].bitcast(F32)
+            bank = psum.tile([P, 512], F32, name="bank", tag="bank")
+            for s in range(2):
+                for a in range(2):
+                    col = (2 * half + s) * 256
+                    nc.tensor.transpose(
+                        bank[:, (2 * s + a) * P:(2 * s + a + 1) * P],
+                        a32[:, col + a:col + 256:2],
+                        ident[:],
+                    )
+            nc.scalar.copy(
+                out=g32.rearrange("q (p y x) -> q p y x", p=P, y=2, x=4)[:, :, half, :],
+                in_=bank[:].rearrange("q (x p) -> q p x", x=4),
+            )
+
+        def quant_a(h):
+            acod[h] = two.tile([P, 512], U32, name="acod", tag="acod", align_bytes=64)
+            ascl[h] = two.tile([P, 512], U8, name="ascl", tag="ascl", align_bytes=64)
+            nc.vector.quantize_mx(out=acod[h][:].bitcast(FP8X4), scales=ascl[h][:], in_=agrp[h][:])
+
+        def stage1(j, c0, ncc=1):
+            if c0 == 0:
+                vgrp[j] = two.tile([P, 2048], BF16, name="vgrp", tag="vgrp", align_bytes=64)
+            banks = {}
+            for cc in range(c0, c0 + ncc):
+                banks[cc] = psum.tile([P, 512], F32, name="bank", tag="bank")
+            for t in range(4):
+                for cc in range(c0, c0 + ncc):
+                    for g in range(2):
+                        wc = slice(t * 256 + g * P, t * 256 + (g + 1) * P)
+                        tk = slice(g * 512 + cc * P, g * 512 + (cc + 1) * P)
+                        nc.tensor.matmul_mx(
+                            out=banks[cc][:, t * P:(t + 1) * P],
+                            lhsT=wcod[j][:, wc].bitcast(FP8X4),
+                            lhsT_scale=wscl[j][:, wc],
+                            rhs=tcod[:, tk].bitcast(FP8X4),
+                            rhs_scale=tscl[:, tk],
+                            start=(g == 0),
+                            stop=(g == 1),
+                        )
+            for cc in range(c0, c0 + ncc):
+                nc.vector.tensor_tensor(
+                    out=vgrp[j][:, cc * 512:(cc + 1) * 512].rearrange("p (c t) -> p c t", t=4),
+                    in0=banks[cc][:].rearrange("p (t c) -> p c t", t=4),
+                    in1=biasf[:, j * 4:(j + 1) * 4].unsqueeze(1).to_broadcast([P, P, 4]),
+                    op=ADD,
+                )
+
+        def quant_v(j, c0, ncc):
+            if c0 == 0:
+                vcod[j] = two.tile([P, 512], U32, name="vcod", tag="vcod", align_bytes=64)
+                vscl[j] = two.tile([P, 512], U8, name="vscl", tag="vscl", align_bytes=64)
+            nc.vector.quantize_mx(
+                out=vcod[j][:, c0 * P:(c0 + ncc) * P].bitcast(FP8X4),
+                scales=vscl[j][:, c0 * P:(c0 + ncc) * P],
+                in_=vgrp[j][:, c0 * 512:(c0 + ncc) * 512],
+            )
+
+        def stage2(j, cc):
+            h = j // 2
+            if cc == 0:
+                osb[j] = outp.tile([P, 2048], F32, name="osb", tag="osb")
+            bank = psum.tile([P, 512], F32, name="bank", tag="bank")
+            vc = slice(cc * P, (cc + 1) * P)
+            nc.tensor.matmul_mx(
+                out=bank[:],
+                lhsT=vcod[j][:, vc].bitcast(FP8X4),
+                lhsT_scale=vscl[j][:, vc],
+                rhs=acod[h][:].bitcast(FP8X4),
+                rhs_scale=ascl[h][:],
+                start=True,
+                stop=True,
+            )
+            nc.scalar.copy(out=osb[j][:, cc * 512:(cc + 1) * 512], in_=bank[:])
+
+        def store(j, c0, ncc):
+            cols = slice(c0 * 512, (c0 + ncc) * 512)
+            nc.sync.dma_start(out=out_v[j // 2, j % 2][:, cols], in_=osb[j][:, cols])
+
+        trans_w(0)
+        for t in range(4):
+            quant_w(0, t, 1)
+        stage1(0, 0, 3)
+        trans_w(1)
+        trans_a(0, 0)
+        trans_a(0, 1)
+        quant_w(1, 0, 2)
+        stage1(0, 3)
+        quant_w(1, 2, 2)
+        quant_a(0)
+
+        for i in range(6):
+            jt = i + 2
+            js = i + 1
+            trans_w(jt)
+            if jt % 2 == 1:
+                trans_a(jt // 2, 0)
+                trans_a(jt // 2, 1)
+            if i == 0:
+                quant_v(0, 0, 4)
+            quant_w(jt, 0, 2)
+            for cc in range(4):
+                stage1(js, cc)
+                if cc == 0 and i == 5:
+                    quant_w(jt, 2, 2)
+                if cc == 1 and jt % 2 == 1:
+                    quant_a(jt // 2)
+                if cc == 2:
+                    quant_v(js, 0, 2)
+                stage2(i, cc)
+                if cc == 1 and i == 5:
+                    store(i, 0, 2)
+            if i < 5:
+                quant_w(jt, 2, 2)
+                quant_v(js, 2, 2)
+                store(i, 0, 4)
+            else:
+                store(i, 2, 2)
+
+        stage1(7, 0)
+        quant_v(6, 2, 2)
+        stage2(6, 0)
+        store(6, 0, 1)
+        stage1(7, 1)
+        stage2(6, 1)
+        store(6, 1, 1)
+        quant_v(7, 0, 1)
+        stage1(7, 2)
+        stage2(6, 2)
+        store(6, 2, 1)
+        quant_v(7, 1, 1)
+        stage1(7, 3)
+        stage2(6, 3)
+        store(6, 3, 1)
+        quant_v(7, 2, 1)
+        stage2(7, 0)
+        store(7, 0, 1)
+        stage2(7, 1)
+        store(7, 1, 1)
+        quant_v(7, 3, 1)
+        stage2(7, 2)
+        store(7, 2, 1)
+        stage2(7, 3)
+        store(7, 3, 1)

@@ -16,9 +16,9 @@ FLOPS = 2 * 4096 * 1024 * 512 + 2 * 4 * 1024 * 512 * 512
 
 def tile_selfattention_pb_kernel(tc, attn, tokens, Wv, bv, out):
     nc = tc.nc
-    tok_v = tokens.rearrange("(g q s) c -> g q (s c)", g=2, q=P, s=4)
-    w_v = Wv.rearrange("(p u e j) k -> j u p e k", u=2, p=P, e=2, j=8)
-    attn_v = attn.rearrange("h (p s) m -> h p (s m)", s=4)
+    tok_v = tokens.rearrange("(g q t) c -> g q (t c)", g=2, q=P, t=4)
+    w_v = Wv.rearrange("(p t j) k -> j p t k", p=P, t=4, j=8)
+    attn_v = attn.rearrange("h (p r) m -> h p (r m)", r=4)
     bv_v = bv.rearrange("(p x) -> p x", p=P, x=32)
     out_v = out.rearrange("h (d i c) l -> h d i (c l)", d=2, i=P, c=4)
 
@@ -32,44 +32,43 @@ def tile_selfattention_pb_kernel(tc, attn, tokens, Wv, bv, out):
         ctx.enter_context(tc.manual_schedule())
 
         braw = keep.tile([P, 32], BF16, name="braw")
-        nc.scalar.dma_start(out=braw[:], in_=bv_v)
         traw = keep.tile([P, 4096], BF16, name="traw")
-        for g in range(2):
-            nc.sync.dma_start(
-                out=traw[:, g * 2048:(g + 1) * 2048],
-                in_=tok_v[g],
-            )
         wraw = {}
         araw = {}
 
-        def load_w(j):
-            wraw[j] = wraw_pool.tile([P, 4096], BF16, name="wraw", tag="wraw")
-            for u in range(2):
-                if j == 0:
-                    for e in range(2):
-                        t = 2 * u + e
-                        nc.sync.dma_start(out=wraw[j][:, t * 1024:(t + 1) * 1024], in_=w_v[j, u][:, e, :])
-                else:
-                    nc.sync.dma_start(
-                        out=wraw[j][:, u * 2048:(u + 1) * 2048].rearrange("p (e k) -> p e k", e=2),
-                        in_=w_v[j, u],
-                    )
+        def load_w(j, t0, nt):
+            if t0 == 0:
+                wraw[j] = wraw_pool.tile([P, 4096], BF16, name="wraw", tag="wraw")
+            nc.sync.dma_start(
+                out=wraw[j][:, t0 * 1024:(t0 + nt) * 1024].rearrange("p (t k) -> p t k", t=nt),
+                in_=w_v[j][:, t0:t0 + nt],
+            )
+
+        def load_t(g):
+            nc.sync.dma_start(out=traw[:, g * 2048:(g + 1) * 2048], in_=tok_v[g])
 
         def load_a(h):
             araw[h] = araw_pool.tile([P, 2048], BF16, name="araw", tag="araw")
             nc.sync.dma_start(out=araw[h][:], in_=attn_v[h])
 
-        load_w(0)
-        load_w(1)
+        nc.scalar.dma_start(out=braw[:], in_=bv_v)
+        load_w(0, 0, 1)
+        load_w(0, 1, 1)
+        load_t(0)
+        load_t(1)
+        load_w(0, 2, 1)
+        load_w(0, 3, 1)
+        load_w(1, 0, 2)
+        load_w(1, 2, 2)
         load_a(0)
-        load_w(2)
-        load_w(3)
+        load_w(2, 0, 4)
+        load_w(3, 0, 4)
         load_a(1)
-        load_w(4)
-        load_w(5)
+        load_w(4, 0, 4)
+        load_w(5, 0, 4)
         load_a(2)
-        load_w(6)
-        load_w(7)
+        load_w(6, 0, 4)
+        load_w(7, 0, 4)
         load_a(3)
 
         ident = keep.tile([P, P], F32, name="ident")
@@ -78,6 +77,7 @@ def tile_selfattention_pb_kernel(tc, attn, tokens, Wv, bv, out):
         tgrp = keep.tile([P, 4096], BF16, name="tgrp", align_bytes=64)
         tcod = keep.tile([P, 1024], U32, name="tcod", align_bytes=64)
         tscl = keep.tile([P, 1024], U8, name="tscl", align_bytes=64)
+
         def regroup(copy, g, k0, nk):
             copy(
                 out=tgrp[:, g * 2048 + k0 * 512:g * 2048 + (k0 + nk) * 512].rearrange(
@@ -86,24 +86,20 @@ def tile_selfattention_pb_kernel(tc, attn, tokens, Wv, bv, out):
                     "q (t i k) -> q k i t", t=4, i=P, k=4)[:, k0:k0 + nk],
             )
 
-        regroup(nc.vector.tensor_copy, 0, 0, 4)
-        regroup(nc.vector.tensor_copy, 1, 0, 2)
-        regroup(nc.scalar.copy, 1, 2, 2)
-        for g in range(2):
+        def quant_t(g):
             nc.vector.quantize_mx(
                 out=tcod[:, g * 512:(g + 1) * 512].bitcast(FP8X4),
                 scales=tscl[:, g * 512:(g + 1) * 512],
                 in_=tgrp[:, g * 2048:(g + 1) * 2048],
             )
-        biasf = keep.tile([P, 32], F32, name="biasf")
-        nc.vector.tensor_copy(
-            out=biasf[:].rearrange("p (j t) -> p j t", t=4),
-            in_=braw[:].rearrange("p (t j) -> p j t", t=4),
-        )
 
+        biasf = keep.tile([P, 32], F32, name="biasf")
+
+        wsep = {}
         wgrp = {}
         wcod = {}
         wscl = {}
+        asep = {}
         agrp = {}
         acod = {}
         ascl = {}
@@ -112,19 +108,38 @@ def tile_selfattention_pb_kernel(tc, attn, tokens, Wv, bv, out):
         vscl = {}
         osb = {}
 
-        def trans_w(j):
-            wgrp[j] = two.tile([P, 4096], BF16, name="wgrp", tag="wgrp", align_bytes=64)
+        def sep_w(j, u):
+            if u == 0:
+                wsep[j] = two.tile([P, 2048], F32, name="wsep", tag="wsep", align_bytes=64)
+            cols = slice(u * 1024, (u + 1) * 1024)
+            nc.vector.tensor_copy(
+                out=wsep[j][:, cols].rearrange("p (b a q) -> p b a q", a=2, q=P),
+                in_=wraw[j][:].bitcast(F32)[:, cols].rearrange("p (b q a) -> p b a q", a=2, q=P),
+            )
+
+        def sep_a(h, half):
+            if half == 0:
+                asep[h] = two.tile([P, 1024], F32, name="asep", tag="asep", align_bytes=64)
+            cols = slice(half * 512, (half + 1) * 512)
+            nc.scalar.copy(
+                out=asep[h][:, cols].rearrange("p (b a q) -> p b a q", a=2, q=P),
+                in_=araw[h][:].bitcast(F32)[:, cols].rearrange("p (b q a) -> p b a q", a=2, q=P),
+            )
+
+        def trans_w(j, t0=0, nt=4):
+            if t0 == 0:
+                wgrp[j] = two.tile([P, 4096], BF16, name="wgrp", tag="wgrp", align_bytes=64)
             w32 = wraw[j][:].bitcast(F32)
             g32 = wgrp[j][:].bitcast(F32)
-            for t in range(4):
+            for t in range(t0, t0 + nt):
                 bank = psum.tile([P, 512], F32, name="bank", tag="bank")
                 for x in range(4):
                     w0 = t * 512 + (x // 2) * 256
-                    nc.tensor.transpose(
-                        bank[:, x * P:(x + 1) * P],
-                        w32[:, w0 + x % 2:w0 + 256:2],
-                        ident[:],
-                    )
+                    if j in wsep:
+                        words = wsep[j][:, w0 + (x % 2) * P:w0 + (x % 2 + 1) * P]
+                    else:
+                        words = w32[:, w0 + x % 2:w0 + 256:2]
+                    nc.tensor.transpose(bank[:, x * P:(x + 1) * P], words, ident[:])
                 nc.scalar.copy(
                     out=g32[:, t * 512:(t + 1) * 512].rearrange("p (g c a) -> p g c a", g=2, c=P, a=2),
                     in_=bank[:].rearrange("p (g a c) -> p g c a", g=2, a=2, c=P),
@@ -146,14 +161,14 @@ def tile_selfattention_pb_kernel(tc, attn, tokens, Wv, bv, out):
             a32 = araw[h][:].bitcast(F32)
             g32 = agrp[h][:].bitcast(F32)
             bank = psum.tile([P, 512], F32, name="bank", tag="bank")
-            for s in range(2):
+            for r in range(2):
                 for a in range(2):
-                    col = (2 * half + s) * 256
-                    nc.tensor.transpose(
-                        bank[:, (2 * s + a) * P:(2 * s + a + 1) * P],
-                        a32[:, col + a:col + 256:2],
-                        ident[:],
-                    )
+                    col = (2 * half + r) * 256
+                    if h in asep:
+                        words = asep[h][:, col + a * P:col + (a + 1) * P]
+                    else:
+                        words = a32[:, col + a:col + 256:2]
+                    nc.tensor.transpose(bank[:, (2 * r + a) * P:(2 * r + a + 1) * P], words, ident[:])
             nc.scalar.copy(
                 out=g32.rearrange("q (p y x) -> q p y x", p=P, y=2, x=4)[:, :, half, :],
                 in_=bank[:].rearrange("q (x p) -> q p x", x=4),
@@ -164,33 +179,29 @@ def tile_selfattention_pb_kernel(tc, attn, tokens, Wv, bv, out):
             ascl[h] = two.tile([P, 512], U8, name="ascl", tag="ascl", align_bytes=64)
             nc.vector.quantize_mx(out=acod[h][:].bitcast(FP8X4), scales=ascl[h][:], in_=agrp[h][:])
 
-        def stage1(j, c0, ncc=1):
-            if c0 == 0:
+        def stage1(j, cc):
+            if cc == 0:
                 vgrp[j] = two.tile([P, 2048], BF16, name="vgrp", tag="vgrp", align_bytes=64)
-            banks = {}
-            for cc in range(c0, c0 + ncc):
-                banks[cc] = psum.tile([P, 512], F32, name="bank", tag="bank")
+            bank = psum.tile([P, 512], F32, name="bank", tag="bank")
             for t in range(4):
-                for cc in range(c0, c0 + ncc):
-                    for g in range(2):
-                        wc = slice(t * 256 + g * P, t * 256 + (g + 1) * P)
-                        tk = slice(g * 512 + cc * P, g * 512 + (cc + 1) * P)
-                        nc.tensor.matmul_mx(
-                            out=banks[cc][:, t * P:(t + 1) * P],
-                            lhsT=wcod[j][:, wc].bitcast(FP8X4),
-                            lhsT_scale=wscl[j][:, wc],
-                            rhs=tcod[:, tk].bitcast(FP8X4),
-                            rhs_scale=tscl[:, tk],
-                            start=(g == 0),
-                            stop=(g == 1),
-                        )
-            for cc in range(c0, c0 + ncc):
-                nc.vector.tensor_tensor(
-                    out=vgrp[j][:, cc * 512:(cc + 1) * 512].rearrange("p (c t) -> p c t", t=4),
-                    in0=banks[cc][:].rearrange("p (t c) -> p c t", t=4),
-                    in1=biasf[:, j * 4:(j + 1) * 4].unsqueeze(1).to_broadcast([P, P, 4]),
-                    op=ADD,
-                )
+                for g in range(2):
+                    wc = slice(t * 256 + g * P, t * 256 + (g + 1) * P)
+                    tk = slice(g * 512 + cc * P, g * 512 + (cc + 1) * P)
+                    nc.tensor.matmul_mx(
+                        out=bank[:, t * P:(t + 1) * P],
+                        lhsT=wcod[j][:, wc].bitcast(FP8X4),
+                        lhsT_scale=wscl[j][:, wc],
+                        rhs=tcod[:, tk].bitcast(FP8X4),
+                        rhs_scale=tscl[:, tk],
+                        start=(g == 0),
+                        stop=(g == 1),
+                    )
+            nc.vector.tensor_tensor(
+                out=vgrp[j][:, cc * 512:(cc + 1) * 512].rearrange("p (c t) -> p c t", t=4),
+                in0=bank[:].rearrange("p (t c) -> p c t", t=4),
+                in1=biasf[:, j * 4:(j + 1) * 4].unsqueeze(1).to_broadcast([P, P, 4]),
+                op=ADD,
+            )
 
         def quant_v(j, c0, ncc):
             if c0 == 0:
@@ -202,7 +213,7 @@ def tile_selfattention_pb_kernel(tc, attn, tokens, Wv, bv, out):
                 in_=vgrp[j][:, c0 * 512:(c0 + ncc) * 512],
             )
 
-        def stage2(j, cc):
+        def stage2(j, cc, copy=nc.scalar.copy):
             h = j // 2
             if cc == 0:
                 osb[j] = outp.tile([P, 2048], F32, name="osb", tag="osb")
@@ -217,22 +228,40 @@ def tile_selfattention_pb_kernel(tc, attn, tokens, Wv, bv, out):
                 start=True,
                 stop=True,
             )
-            nc.scalar.copy(out=osb[j][:, cc * 512:(cc + 1) * 512], in_=bank[:])
+            copy(out=osb[j][:, cc * 512:(cc + 1) * 512], in_=bank[:])
 
         def store(j, c0, ncc):
             cols = slice(c0 * 512, (c0 + ncc) * 512)
             nc.sync.dma_start(out=out_v[j // 2, j % 2][:, cols], in_=osb[j][:, cols])
 
-        trans_w(0)
-        for t in range(4):
-            quant_w(0, t, 1)
-        stage1(0, 0, 3)
+        trans_w(0, 0, 2)
+        quant_w(0, 0, 2)
+        regroup(nc.vector.tensor_copy, 0, 0, 2)
+        regroup(nc.scalar.copy, 0, 2, 2)
+        regroup(nc.vector.tensor_copy, 1, 0, 3)
+        regroup(nc.scalar.copy, 1, 3, 1)
+        quant_t(0)
+        quant_t(1)
+        trans_w(0, 2, 2)
+        quant_w(0, 2, 1)
+        quant_w(0, 3, 1)
+        nc.vector.tensor_copy(
+            out=biasf[:].rearrange("p (j t) -> p j t", t=4),
+            in_=braw[:].rearrange("p (t j) -> p j t", t=4),
+        )
+        stage1(0, 0)
+        stage1(0, 1)
+        stage1(0, 2)
+        stage1(0, 3)
         trans_w(1)
         trans_a(0, 0)
         trans_a(0, 1)
+        sep_w(2, 0)
+        quant_v(0, 0, 2)
         quant_w(1, 0, 2)
-        stage1(0, 3)
+        sep_w(2, 1)
         quant_w(1, 2, 2)
+        quant_v(0, 2, 2)
         quant_a(0)
 
         for i in range(6):
@@ -242,29 +271,32 @@ def tile_selfattention_pb_kernel(tc, attn, tokens, Wv, bv, out):
             if jt % 2 == 1:
                 trans_a(jt // 2, 0)
                 trans_a(jt // 2, 1)
-            if i == 0:
-                quant_v(0, 0, 4)
+            if i < 5:
+                sep_w(jt + 1, 0)
+                sep_w(jt + 1, 1)
             quant_w(jt, 0, 2)
             for cc in range(4):
                 stage1(js, cc)
-                if cc == 0 and i == 5:
+                if i == 5 and cc == 0:
                     quant_w(jt, 2, 2)
                 if cc == 1 and jt % 2 == 1:
                     quant_a(jt // 2)
                 if cc == 2:
                     quant_v(js, 0, 2)
                 stage2(i, cc)
-                if cc == 1 and i == 5:
+                if cc in (0, 2) and jt % 2 == 0:
+                    sep_a(jt // 2, cc // 2)
+                if i == 5 and cc == 1:
                     store(i, 0, 2)
             if i < 5:
                 quant_w(jt, 2, 2)
-                quant_v(js, 2, 2)
+            quant_v(js, 2, 2)
+            if i < 5:
                 store(i, 0, 4)
             else:
                 store(i, 2, 2)
 
         stage1(7, 0)
-        quant_v(6, 2, 2)
         stage2(6, 0)
         store(6, 0, 1)
         stage1(7, 1)

@@ -52,16 +52,19 @@ def tile_selfattention_pb_kernel(tc, attn, tokens, Wv, bv, out):
             nc.sync.dma_start(out=araw[h][:], in_=attn_v[h])
 
         nc.scalar.dma_start(out=braw[:], in_=bv_v)
-        load_w(0, 0, 1)
-        load_w(0, 1, 1)
         load_t(0)
         load_t(1)
+        load_w(0, 0, 1)
+        load_w(0, 1, 1)
         load_w(0, 2, 1)
         load_w(0, 3, 1)
-        load_w(1, 0, 2)
-        load_w(1, 2, 2)
+        load_w(1, 0, 1)
+        load_w(1, 1, 1)
+        load_w(1, 2, 1)
+        load_w(1, 3, 1)
+        load_w(2, 0, 2)
+        load_w(2, 2, 2)
         load_a(0)
-        load_w(2, 0, 4)
         load_w(3, 0, 4)
         load_a(1)
         load_w(4, 0, 4)
@@ -234,33 +237,31 @@ def tile_selfattention_pb_kernel(tc, attn, tokens, Wv, bv, out):
             cols = slice(c0 * 512, (c0 + ncc) * 512)
             nc.sync.dma_start(out=out_v[j // 2, j % 2][:, cols], in_=osb[j][:, cols])
 
-        trans_w(0, 0, 2)
-        quant_w(0, 0, 2)
-        regroup(nc.vector.tensor_copy, 0, 0, 2)
-        regroup(nc.scalar.copy, 0, 2, 2)
+        regroup(nc.vector.tensor_copy, 0, 0, 3)
+        regroup(nc.scalar.copy, 0, 3, 1)
         regroup(nc.vector.tensor_copy, 1, 0, 3)
         regroup(nc.scalar.copy, 1, 3, 1)
-        quant_t(0)
-        quant_t(1)
-        trans_w(0, 2, 2)
-        quant_w(0, 2, 1)
-        quant_w(0, 3, 1)
         nc.vector.tensor_copy(
             out=biasf[:].rearrange("p (j t) -> p j t", t=4),
             in_=braw[:].rearrange("p (t j) -> p j t", t=4),
         )
+        quant_t(0)
+        quant_t(1)
+        trans_w(0)
+        quant_w(0, 0, 2)
+        trans_w(1)
+        quant_w(0, 2, 2)
+        quant_w(1, 0, 2)
         stage1(0, 0)
         stage1(0, 1)
+        quant_w(1, 2, 2)
         stage1(0, 2)
+        sep_w(2, 0)
         stage1(0, 3)
-        trans_w(1)
         trans_a(0, 0)
         trans_a(0, 1)
-        sep_w(2, 0)
-        quant_v(0, 0, 2)
-        quant_w(1, 0, 2)
         sep_w(2, 1)
-        quant_w(1, 2, 2)
+        quant_v(0, 0, 2)
         quant_v(0, 2, 2)
         quant_a(0)
 

@@ -77,6 +77,12 @@ def tile_selfattention_pb_kernel(tc, attn, tokens, Wv, bv, out):
         ident = keep.tile([P, P], F32, name="ident")
         make_identity(nc, ident[:])
 
+        warm = keep.tile([P, 512], BF16, name="warm")
+        nc.vector.memset(warm[:], 0.0)
+        warm_bank = psum.tile([P, 512], F32, name="bank", tag="bank")
+        for n in range(10):
+            nc.tensor.matmul(warm_bank[:], lhsT=warm[:, 0:P], rhs=warm[:], start=True, stop=True)
+
         tgrp = keep.tile([P, 4096], BF16, name="tgrp", align_bytes=64)
         tcod = keep.tile([P, 1024], U32, name="tcod", align_bytes=64)
         tscl = keep.tile([P, 1024], U8, name="tscl", align_bytes=64)
@@ -233,14 +239,31 @@ def tile_selfattention_pb_kernel(tc, attn, tokens, Wv, bv, out):
             )
             copy(out=osb[j][:, cc * 512:(cc + 1) * 512], in_=bank[:])
 
+        def stage2_half(j, cc, half, copy):
+            h = j // 2
+            bank = psum.tile([P, 512], F32, name="bank", tag="bank")
+            vc = slice(cc * P, (cc + 1) * P)
+            lc = slice(half * 256, (half + 1) * 256)
+            cols = slice(cc * 512 + half * 256, cc * 512 + (half + 1) * 256)
+            nc.tensor.matmul_mx(
+                out=bank[:, 0:256],
+                lhsT=vcod[j][:, vc].bitcast(FP8X4),
+                lhsT_scale=vscl[j][:, vc],
+                rhs=acod[h][:, lc].bitcast(FP8X4),
+                rhs_scale=ascl[h][:, lc],
+                start=True,
+                stop=True,
+            )
+            copy(out=osb[j][:, cols], in_=bank[:, 0:256])
+            nc.sync.dma_start(out=out_v[j // 2, j % 2][:, cols], in_=osb[j][:, cols])
+
         def store(j, c0, ncc):
             cols = slice(c0 * 512, (c0 + ncc) * 512)
             nc.sync.dma_start(out=out_v[j // 2, j % 2][:, cols], in_=osb[j][:, cols])
 
-        regroup(nc.vector.tensor_copy, 0, 0, 3)
-        regroup(nc.scalar.copy, 0, 3, 1)
-        regroup(nc.vector.tensor_copy, 1, 0, 3)
-        regroup(nc.scalar.copy, 1, 3, 1)
+        regroup(nc.vector.tensor_copy, 0, 0, 4)
+        regroup(nc.vector.tensor_copy, 1, 0, 2)
+        regroup(nc.scalar.copy, 1, 2, 2)
         nc.vector.tensor_copy(
             out=biasf[:].rearrange("p (j t) -> p j t", t=4),
             in_=braw[:].rearrange("p (t j) -> p j t", t=4),
@@ -314,10 +337,10 @@ def tile_selfattention_pb_kernel(tc, attn, tokens, Wv, bv, out):
         quant_v(7, 2, 1)
         stage2(7, 0)
         store(7, 0, 1)
-        stage2(7, 1)
-        store(7, 1, 1)
         quant_v(7, 3, 1)
+        stage2(7, 1, nc.vector.tensor_copy)
+        store(7, 1, 1)
         stage2(7, 2)
         store(7, 2, 1)
-        stage2(7, 3)
-        store(7, 3, 1)
+        stage2_half(7, 3, 0, nc.vector.tensor_copy)
+        stage2_half(7, 3, 1, nc.scalar.copy)

@@ -117,11 +117,11 @@ def tile_selfattention_pb_kernel(tc, attn, tokens, Wv, bv, out):
         vscl = {}
         osb = {}
 
-        def sep_w(j, u):
-            if u == 0:
+        def sep_w(j, t0, nt, copy):
+            if t0 == 0:
                 wsep[j] = two.tile([P, 2048], F32, name="wsep", tag="wsep", align_bytes=64)
-            cols = slice(u * 1024, (u + 1) * 1024)
-            nc.vector.tensor_copy(
+            cols = slice(t0 * 512, (t0 + nt) * 512)
+            copy(
                 out=wsep[j][:, cols].rearrange("p (b a q) -> p b a q", a=2, q=P),
                 in_=wraw[j][:].bitcast(F32)[:, cols].rearrange("p (b q a) -> p b a q", a=2, q=P),
             )
@@ -272,21 +272,21 @@ def tile_selfattention_pb_kernel(tc, attn, tokens, Wv, bv, out):
         quant_t(1)
         trans_w(0)
         quant_w(0, 0, 2)
-        trans_w(1)
         quant_w(0, 2, 2)
+        trans_w(1)
         quant_w(1, 0, 2)
         stage1(0, 0)
         stage1(0, 1)
         quant_w(1, 2, 2)
         stage1(0, 2)
-        sep_w(2, 0)
+        sep_w(2, 0, 2, nc.gpsimd.tensor_copy)
         stage1(0, 3)
         trans_a(0, 0)
         trans_a(0, 1)
-        sep_w(2, 1)
+        sep_w(2, 2, 2, nc.gpsimd.tensor_copy)
         quant_v(0, 0, 2)
-        quant_v(0, 2, 2)
         quant_a(0)
+        quant_v(0, 2, 2)
 
         for i in range(6):
             jt = i + 2
@@ -296,25 +296,34 @@ def tile_selfattention_pb_kernel(tc, attn, tokens, Wv, bv, out):
                 trans_a(jt // 2, 0)
                 trans_a(jt // 2, 1)
             if i < 5:
-                sep_w(jt + 1, 0)
-                sep_w(jt + 1, 1)
-            quant_w(jt, 0, 2)
+                sep_w(jt + 1, 0, 2, nc.vector.tensor_copy)
+            if i > 0:
+                quant_v(i, 2, 2)
+            if i < 5:
+                sep_w(jt + 1, 2, 2, nc.vector.tensor_copy)
+                quant_w(jt, 0, 2)
             for cc in range(4):
                 stage1(js, cc)
                 if i == 5 and cc == 0:
+                    quant_w(jt, 0, 2)
+                if i == 5 and cc == 1:
                     quant_w(jt, 2, 2)
+                    quant_v(js, 0, 2)
                 if cc == 1 and jt % 2 == 1:
                     quant_a(jt // 2)
-                if cc == 2:
+                if cc == 2 and i < 5:
+                    quant_w(jt, 2, 2)
                     quant_v(js, 0, 2)
-                stage2(i, cc)
+                if cc >= 0:
+                    stage2(i, cc - 0)
                 if cc in (0, 2) and jt % 2 == 0:
                     sep_a(jt // 2, cc // 2)
-                if i == 5 and cc == 1:
+                if i == 5 and cc == 0 + 1:
                     store(i, 0, 2)
-            if i < 5:
-                quant_w(jt, 2, 2)
-            quant_v(js, 2, 2)
+            for cc in range(4 - 0, 4):
+                stage2(i, cc)
+            if i == 5:
+                quant_v(js, 2, 2)
             if i < 5:
                 store(i, 0, 4)
             else:

@@ -126,11 +126,11 @@ def tile_selfattention_pb_kernel(tc, attn, tokens, Wv, bv, out):
                 in_=wraw[j][:].bitcast(F32)[:, cols].rearrange("p (b q a) -> p b a q", a=2, q=P),
             )
 
-        def sep_a(h, half):
+        def sep_a(h, half, copy):
             if half == 0:
                 asep[h] = two.tile([P, 1024], F32, name="asep", tag="asep", align_bytes=64)
             cols = slice(half * 512, (half + 1) * 512)
-            nc.scalar.copy(
+            copy(
                 out=asep[h][:, cols].rearrange("p (b a q) -> p b a q", a=2, q=P),
                 in_=araw[h][:].bitcast(F32)[:, cols].rearrange("p (b q a) -> p b a q", a=2, q=P),
             )
@@ -292,9 +292,9 @@ def tile_selfattention_pb_kernel(tc, attn, tokens, Wv, bv, out):
             jt = i + 2
             js = i + 1
             trans_w(jt)
-            if jt % 2 == 1:
-                trans_a(jt // 2, 0)
-                trans_a(jt // 2, 1)
+            if i in (1, 3, 4):
+                trans_a((i + 2) // 2, 0)
+                trans_a((i + 2) // 2, 1)
             if i < 5:
                 sep_w(jt + 1, 0, 2, nc.vector.tensor_copy)
             if i > 0:
@@ -309,15 +309,15 @@ def tile_selfattention_pb_kernel(tc, attn, tokens, Wv, bv, out):
                 if i == 5 and cc == 1:
                     quant_w(jt, 2, 2)
                     quant_v(js, 0, 2)
-                if cc == 1 and jt % 2 == 1:
-                    quant_a(jt // 2)
+                if (i, cc) in ((1, 1), (3, 1), (4, 3)):
+                    quant_a((i + 2) // 2)
                 if cc == 2 and i < 5:
                     quant_w(jt, 2, 2)
                     quant_v(js, 0, 2)
                 if cc >= 0:
                     stage2(i, cc - 0)
-                if cc in (0, 2) and jt % 2 == 0:
-                    sep_a(jt // 2, cc // 2)
+                if cc in (0, 2) and i in (0, 2, 3):
+                    sep_a((i + 3) // 2, cc // 2, nc.scalar.copy if i == 3 else nc.scalar.copy)
                 if i == 5 and cc == 0 + 1:
                     store(i, 0, 2)
             for cc in range(4 - 0, 4):

from contextlib import ExitStack

import concourse.mybir as mybir
from concourse.masks import make_identity

F32 = mybir.dt.float32
BF16 = mybir.dt.bfloat16
U32 = mybir.dt.uint32
U8 = mybir.dt.uint8
FP8X4 = mybir.dt.float8_e4m3fn_x4
ADD = mybir.AluOpType.add

P = 128
FLOPS = 2 * 4096 * 1024 * 512 + 2 * 4 * 1024 * 512 * 512


def tile_selfattention_pb_kernel(tc, attn, tokens, Wv, bv, out):
    nc = tc.nc
    tok_v = tokens.rearrange("(g q t) c -> g q (t c)", g=2, q=P, t=4)
    w_v = Wv.rearrange("(p t j) k -> j p t k", p=P, t=4, j=8)
    attn_v = attn.rearrange("h (p r) m -> h p (r m)", r=4)
    bv_v = bv.rearrange("(p x) -> p x", p=P, x=32)
    out_v = out.rearrange("h (d i c) l -> h d i (c l)", d=2, i=P, c=4)

    with ExitStack() as ctx:
        keep = ctx.enter_context(tc.tile_pool(name="keep", bufs=1))
        wraw_pool = ctx.enter_context(tc.tile_pool(name="wraw", bufs=8))
        araw_pool = ctx.enter_context(tc.tile_pool(name="araw", bufs=4))
        two = ctx.enter_context(tc.tile_pool(name="two", bufs=2))
        outp = ctx.enter_context(tc.tile_pool(name="outp", bufs=3))
        psum = ctx.enter_context(tc.psum_pool(name="psum", bufs=8))
        ctx.enter_context(tc.manual_schedule())

        braw = keep.tile([P, 32], BF16, name="braw")
        traw = keep.tile([P, 4096], BF16, name="traw")
        wraw = {}
        araw = {}

        def load_w(j, t0, nt):
            if t0 == 0:
                wraw[j] = wraw_pool.tile([P, 4096], BF16, name="wraw", tag="wraw")
            nc.sync.dma_start(
                out=wraw[j][:, t0 * 1024:(t0 + nt) * 1024].rearrange("p (t k) -> p t k", t=nt),
                in_=w_v[j][:, t0:t0 + nt],
            )

        def load_t(g):
            nc.sync.dma_start(out=traw[:, g * 2048:(g + 1) * 2048], in_=tok_v[g])

        def load_a(h):
            araw[h] = araw_pool.tile([P, 2048], BF16, name="araw", tag="araw")
            nc.sync.dma_start(out=araw[h][:], in_=attn_v[h])

        nc.scalar.dma_start(out=braw[:], in_=bv_v)
        load_t(0)
        load_t(1)
        load_w(0, 0, 1)
        load_w(0, 1, 1)
        load_w(0, 2, 1)
        load_w(0, 3, 1)
        load_w(1, 0, 1)
        load_w(1, 1, 1)
        load_w(1, 2, 1)
        load_w(1, 3, 1)
        load_w(2, 0, 2)
        load_w(2, 2, 2)
        load_a(0)
        load_w(3, 0, 4)
        load_a(1)
        load_w(4, 0, 4)
        load_w(5, 0, 4)
        load_a(2)
        load_w(6, 0, 4)
        load_w(7, 0, 4)
        load_a(3)

        ident = keep.tile([P, P], F32, name="ident")
        make_identity(nc, ident[:])

        warm = keep.tile([P, 512], BF16, name="warm")
        nc.vector.memset(warm[:], 0.0)
        warm_bank = psum.tile([P, 512], F32, name="bank", tag="bank")
        for n in range(10):
            nc.tensor.matmul(warm_bank[:], lhsT=warm[:, 0:P], rhs=warm[:], start=True, stop=True)

        tgrp = keep.tile([P, 4096], BF16, name="tgrp", align_bytes=64)
        tcod = keep.tile([P, 1024], U32, name="tcod", align_bytes=64)
        tscl = keep.tile([P, 1024], U8, name="tscl", align_bytes=64)

        def regroup(copy, g, k0, nk):
            copy(
                out=tgrp[:, g * 2048 + k0 * 512:g * 2048 + (k0 + nk) * 512].rearrange(
                    "q (k i t) -> q k i t", k=nk, i=P, t=4),
                in_=traw[:, g * 2048:(g + 1) * 2048].rearrange(
                    "q (t i k) -> q k i t", t=4, i=P, k=4)[:, k0:k0 + nk],
            )

        def quant_t(g):
            nc.vector.quantize_mx(
                out=tcod[:, g * 512:(g + 1) * 512].bitcast(FP8X4),
                scales=tscl[:, g * 512:(g + 1) * 512],
                in_=tgrp[:, g * 2048:(g + 1) * 2048],
            )

        biasf = keep.tile([P, 32], F32, name="biasf")

        wsep = {}
        wgrp = {}
        wcod = {}
        wscl = {}
        asep = {}
        agrp = {}
        acod = {}
        ascl = {}
        vgrp = {}
        vcod = {}
        vscl = {}
        osb = {}

        def sep_w(j, t0, nt, copy):
            if t0 == 0:
                wsep[j] = two.tile([P, 2048], F32, name="wsep", tag="wsep", align_bytes=64)
            cols = slice(t0 * 512, (t0 + nt) * 512)
            copy(
                out=wsep[j][:, cols].rearrange("p (b a q) -> p b a q", a=2, q=P),
                in_=wraw[j][:].bitcast(F32)[:, cols].rearrange("p (b q a) -> p b a q", a=2, q=P),
            )

        def sep_a(h, half, copy):
            if half == 0:
                asep[h] = two.tile([P, 1024], F32, name="asep", tag="asep", align_bytes=64)
            cols = slice(half * 512, (half + 1) * 512)
            copy(
                out=asep[h][:, cols].rearrange("p (b a q) -> p b a q", a=2, q=P),
                in_=araw[h][:].bitcast(F32)[:, cols].rearrange("p (b q a) -> p b a q", a=2, q=P),
            )

        def trans_w(j, t0=0, nt=4):
            if t0 == 0:
                wgrp[j] = two.tile([P, 4096], BF16, name="wgrp", tag="wgrp", align_bytes=64)
            w32 = wraw[j][:].bitcast(F32)
            g32 = wgrp[j][:].bitcast(F32)
            for t in range(t0, t0 + nt):
                bank = psum.tile([P, 512], F32, name="bank", tag="bank")
                for x in range(4):
                    w0 = t * 512 + (x // 2) * 256
                    if j in wsep:
                        words = wsep[j][:, w0 + (x % 2) * P:w0 + (x % 2 + 1) * P]
                    else:
                        words = w32[:, w0 + x % 2:w0 + 256:2]
                    nc.tensor.transpose(bank[:, x * P:(x + 1) * P], words, ident[:])
                nc.scalar.copy(
                    out=g32[:, t * 512:(t + 1) * 512].rearrange("p (g c a) -> p g c a", g=2, c=P, a=2),
                    in_=bank[:].rearrange("p (g a c) -> p g c a", g=2, a=2, c=P),
                )

        def quant_w(j, t0, nt):
            if t0 == 0:
                wcod[j] = two.tile([P, 1024], U32, name="wcod", tag="wcod", align_bytes=64)
                wscl[j] = two.tile([P, 1024], U8, name="wscl", tag="wscl", align_bytes=64)
            nc.vector.quantize_mx(
                out=wcod[j][:, t0 * 256:(t0 + nt) * 256].bitcast(FP8X4),
                scales=wscl[j][:, t0 * 256:(t0 + nt) * 256],
                in_=wgrp[j][:, t0 * 1024:(t0 + nt) * 1024],
            )

        def trans_a(h, half):
            if half == 0:
                agrp[h] = two.tile([P, 2048], BF16, name="agrp", tag="agrp", align_bytes=64)
            a32 = araw[h][:].bitcast(F32)
            g32 = agrp[h][:].bitcast(F32)
            bank = psum.tile([P, 512], F32, name="bank", tag="bank")
            for r in range(2):
                for a in range(2):
                    col = (2 * half + r) * 256
                    if h in asep:
                        words = asep[h][:, col + a * P:col + (a + 1) * P]
                    else:
                        words = a32[:, col + a:col + 256:2]
                    nc.tensor.transpose(bank[:, (2 * r + a) * P:(2 * r + a + 1) * P], words, ident[:])
            nc.scalar.copy(
                out=g32.rearrange("q (p y x) -> q p y x", p=P, y=2, x=4)[:, :, half, :],
                in_=bank[:].rearrange("q (x p) -> q p x", x=4),
            )

        def quant_a(h):
            acod[h] = two.tile([P, 512], U32, name="acod", tag="acod", align_bytes=64)
            ascl[h] = two.tile([P, 512], U8, name="ascl", tag="ascl", align_bytes=64)
            nc.vector.quantize_mx(out=acod[h][:].bitcast(FP8X4), scales=ascl[h][:], in_=agrp[h][:])

        def stage1(j, cc):
            if cc == 0:
                vgrp[j] = two.tile([P, 2048], BF16, name="vgrp", tag="vgrp", align_bytes=64)
            bank = psum.tile([P, 512], F32, name="bank", tag="bank")
            for t in range(4):
                for g in range(2):
                    wc = slice(t * 256 + g * P, t * 256 + (g + 1) * P)
                    tk = slice(g * 512 + cc * P, g * 512 + (cc + 1) * P)
                    nc.tensor.matmul_mx(
                        out=bank[:, t * P:(t + 1) * P],
                        lhsT=wcod[j][:, wc].bitcast(FP8X4),
                        lhsT_scale=wscl[j][:, wc],
                        rhs=tcod[:, tk].bitcast(FP8X4),
                        rhs_scale=tscl[:, tk],
                        start=(g == 0),
                        stop=(g == 1),
                    )
            nc.vector.tensor_tensor(
                out=vgrp[j][:, cc * 512:(cc + 1) * 512].rearrange("p (c t) -> p c t", t=4),
                in0=bank[:].rearrange("p (t c) -> p c t", t=4),
                in1=biasf[:, j * 4:(j + 1) * 4].unsqueeze(1).to_broadcast([P, P, 4]),
                op=ADD,
            )

        def quant_v(j, c0, ncc):
            if c0 == 0:
                vcod[j] = two.tile([P, 512], U32, name="vcod", tag="vcod", align_bytes=64)
                vscl[j] = two.tile([P, 512], U8, name="vscl", tag="vscl", align_bytes=64)
            nc.vector.quantize_mx(
                out=vcod[j][:, c0 * P:(c0 + ncc) * P].bitcast(FP8X4),
                scales=vscl[j][:, c0 * P:(c0 + ncc) * P],
                in_=vgrp[j][:, c0 * 512:(c0 + ncc) * 512],
            )

        def stage2(j, cc, copy=nc.scalar.copy):
            h = j // 2
            if cc == 0:
                osb[j] = outp.tile([P, 2048], F32, name="osb", tag="osb")
            bank = psum.tile([P, 512], F32, name="bank", tag="bank")
            vc = slice(cc * P, (cc + 1) * P)
            nc.tensor.matmul_mx(
                out=bank[:],
                lhsT=vcod[j][:, vc].bitcast(FP8X4),
                lhsT_scale=vscl[j][:, vc],
                rhs=acod[h][:].bitcast(FP8X4),
                rhs_scale=ascl[h][:],
                start=True,
                stop=True,
            )
            copy(out=osb[j][:, cc * 512:(cc + 1) * 512], in_=bank[:])

        def stage2_half(j, cc, half, copy):
            h = j // 2
            bank = psum.tile([P, 512], F32, name="bank", tag="bank")
            vc = slice(cc * P, (cc + 1) * P)
            lc = slice(half * 256, (half + 1) * 256)
            cols = slice(cc * 512 + half * 256, cc * 512 + (half + 1) * 256)
            nc.tensor.matmul_mx(
                out=bank[:, 0:256],
                lhsT=vcod[j][:, vc].bitcast(FP8X4),
                lhsT_scale=vscl[j][:, vc],
                rhs=acod[h][:, lc].bitcast(FP8X4),
                rhs_scale=ascl[h][:, lc],
                start=True,
                stop=True,
            )
            copy(out=osb[j][:, cols], in_=bank[:, 0:256])
            nc.sync.dma_start(out=out_v[j // 2, j % 2][:, cols], in_=osb[j][:, cols])

        def store(j, c0, ncc):
            cols = slice(c0 * 512, (c0 + ncc) * 512)
            nc.sync.dma_start(out=out_v[j // 2, j % 2][:, cols], in_=osb[j][:, cols])

        regroup(nc.vector.tensor_copy, 0, 0, 4)
        regroup(nc.vector.tensor_copy, 1, 0, 2)
        regroup(nc.scalar.copy, 1, 2, 2)
        nc.vector.tensor_copy(
            out=biasf[:].rearrange("p (j t) -> p j t", t=4),
            in_=braw[:].rearrange("p (t j) -> p j t", t=4),
        )
        quant_t(0)
        quant_t(1)
        trans_w(0)
        quant_w(0, 0, 2)
        quant_w(0, 2, 2)
        trans_w(1)
        quant_w(1, 0, 2)
        stage1(0, 0)
        stage1(0, 1)
        quant_w(1, 2, 2)
        stage1(0, 2)
        sep_w(2, 0, 2, nc.gpsimd.tensor_copy)
        stage1(0, 3)
        trans_a(0, 0)
        trans_a(0, 1)
        sep_w(2, 2, 2, nc.gpsimd.tensor_copy)
        quant_v(0, 0, 2)
        quant_a(0)
        quant_v(0, 2, 2)

        for i in range(6):
            jt = i + 2
            js = i + 1
            trans_w(jt)
            if i in (1, 3, 4):
                trans_a((i + 2) // 2, 0)
                trans_a((i + 2) // 2, 1)
            if i < 5:
                sep_w(jt + 1, 0, 2, nc.vector.tensor_copy)
            if i > 0:
                quant_v(i, 2, 2)
            if i < 5:
                sep_w(jt + 1, 2, 2, nc.vector.tensor_copy)
                quant_w(jt, 0, 2)
            for cc in range(4):
                stage1(js, cc)
                if i == 5 and cc == 0:
                    quant_w(jt, 0, 2)
                if i == 5 and cc == 1:
                    quant_w(jt, 2, 2)
                    quant_v(js, 0, 2)
                if (i, cc) in ((1, 1), (3, 1), (4, 3)):
                    quant_a((i + 2) // 2)
                if cc == 2 and i < 5:
                    quant_w(jt, 2, 2)
                    quant_v(js, 0, 2)
                if cc >= 0:
                    stage2(i, cc - 0)
                if cc in (0, 2) and i in (0, 2, 3):
                    sep_a((i + 3) // 2, cc // 2, nc.scalar.copy if i == 3 else nc.scalar.copy)
                if i == 5 and cc == 0 + 1:
                    store(i, 0, 2)
            for cc in range(4 - 0, 4):
                stage2(i, cc)
            if i == 5:
                quant_v(js, 2, 2)
            if i < 5:
                store(i, 0, 4)
            else:
                store(i, 2, 2)

        stage1(7, 0)
        stage2(6, 0)
        store(6, 0, 1)
        stage1(7, 1)
        stage2(6, 1)
        store(6, 1, 1)
        quant_v(7, 0, 1)
        stage1(7, 2)
        stage2(6, 2)
        store(6, 2, 1)
        quant_v(7, 1, 1)
        stage1(7, 3)
        stage2(6, 3)
        store(6, 3, 1)
        quant_v(7, 2, 1)
        stage2(7, 0)
        store(7, 0, 1)
        quant_v(7, 3, 1)
        stage2(7, 1, nc.vector.tensor_copy)
        store(7, 1, 1)
        stage2(7, 2)
        store(7, 2, 1)
        stage2_half(7, 3, 0, nc.vector.tensor_copy)
        stage2_half(7, 3, 1, nc.scalar.copy)
